import numpy as np
import ml_dtypes


def mxq(x, axis, fmt="e4m3"):
    dtype, down = {"e4m3": (ml_dtypes.float8_e4m3fn, 7), "e5m2": (ml_dtypes.float8_e5m2, 14)}[fmt]
    v = np.moveaxis(np.asarray(x, np.float32).astype(ml_dtypes.bfloat16).astype(np.float64), axis, -1)
    blocks = v.reshape(v.shape[:-1] + (-1, 32))
    amax = np.abs(blocks).max(-1, keepdims=True)
    byte = np.maximum(np.where(amax > 0, np.frexp(amax)[1] - 1 + 127, 0) - down, 1)
    scale = np.exp2(byte - 127.0)
    codes = (blocks / scale).astype(np.float32).astype(dtype).astype(np.float64)
    return np.moveaxis((codes * scale).reshape(v.shape), -1, axis)


WIDE = False


def mx_kscale(k):
    if not WIDE:
        return np.ones(k)
    levels = np.array([10, -10, 5, -5, 0])
    if k % 512:
        return np.exp2(np.random.permutation(np.resize(levels, k // 32))).repeat(32)
    a = np.empty((k // 512, 16))
    for p in range(k // 512):
        a[p, :8] = np.random.permutation(np.resize(levels, 8))
        for g in range(8):
            far = levels[np.abs(levels - a[p, g]) >= 10]
            a[p, g + 8] = far[np.random.randint(len(far))]
    return np.exp2(a.ravel()).repeat(32)


BF16 = ml_dtypes.bfloat16


def bf(x):
    return np.asarray(x, np.float32).astype(BF16)


def f64(x):
    return np.asarray(x).astype(np.float64)


B, N, C = 1, 2048, 512
Q = N ** 0.25


def setup_inputs():
    s = mx_kscale(B * N).reshape(B, N, 1)
    u = mx_kscale(C)
    msg = bf((1.4 * np.random.standard_normal((B, 1, C)) + 1.2 * np.random.standard_normal((B, N, C))) / Q)
    A = bf(np.random.uniform(0.0, 1.0, (B, N, N)) * 2.0 / N ** 0.75)
    h0 = bf(np.maximum(np.random.standard_normal((B, N, C)) * 1.35, 0.0))
    Ws0 = bf(np.random.uniform(-1.0, 1.0, (C, C)) * 1.5 / np.sqrt(C))
    b = bf(np.random.uniform(-1.0, 1.0, C) * 0.5)
    g = bf(np.random.standard_normal((B, N, C)) * np.exp2(np.random.randint(-6, 1, (B, N, 1))) * 4.0 / s * u)
    z = f64(A) @ f64(msg) + f64(h0) @ f64(Ws0).T + f64(b)
    return {"A": A, "msg": msg, "h": bf(f64(h0) * s), "Ws": bf(f64(Ws0) / u[:, None]), "b": b,
            "z": np.asarray(z, np.float32), "grad_out": g}


def reference(A, msg, h, Ws, b, z, grad_out):
    dz = f64(grad_out) * (f64(z) > 0.0)
    dz2 = dz.reshape(B * N, C)
    h2 = f64(h).reshape(B * N, C)
    dh = (mxq(dz2, 1, "e5m2") @ mxq(f64(Ws), 0, "e4m3")).reshape(B, N, C)
    dWs = mxq(dz2, 0, "e5m2").T @ mxq(h2, 0, "e4m3")
    return dh, dWs

@@ -1,0 +1,202 @@
+from contextlib import ExitStack
+
+import concourse.mybir as mybir
+from concourse.masks import make_identity
+
+NODES = 2048
+CH = 512
+FLOPS = 2 * 2 * NODES * CH * CH
+BYTES = NODES * CH * (2 + 4 + 2) + CH * CH * 2 + NODES * CH * 4 + CH * CH * 4
+
+F32 = mybir.dt.float32
+BF16 = mybir.dt.bfloat16
+U32 = mybir.dt.uint32
+U8 = mybir.dt.uint8
+E4 = mybir.dt.float8_e4m3fn_x4
+E5 = mybir.dt.float8_e5m2_x4
+ALU = mybir.AluOpType
+
+P = 128
+PACK = 4
+PASS = P * PACK
+NCH = NODES // PASS
+HALF = CH // 2
+
+
+def tile_gcnstacking_pb_v_kernel(tc, A, msg, h, Ws, b, z, grad_out, out_0, out_1):
+    nc = tc.nc
+    z_v = z.flatten_outer_dims().rearrange("(c p j) w -> p c j w", p=P, j=PACK)
+    g_v = grad_out.flatten_outer_dims().rearrange("(c p j) w -> p c j w", p=P, j=PACK)
+    h_v = h.flatten_outer_dims().rearrange("(c p j) w -> p c j w", p=P, j=PACK)
+    o0_v = out_0.flatten_outer_dims().rearrange("(c p j) w -> p c j w", p=P, j=PACK)
+    w_v = Ws.rearrange("(p j) i -> p j i", j=PACK)
+    o1_v = out_1.rearrange("(t m) i -> m t i", m=P)
+
+    with ExitStack() as ctx:
+        raw = ctx.enter_context(tc.tile_pool(name="raw", bufs=1))
+        keep = ctx.enter_context(tc.tile_pool(name="keep", bufs=1))
+        rot = ctx.enter_context(tc.tile_pool(name="rot", bufs=2))
+        accp = ctx.enter_context(tc.psum_pool(name="accp", bufs=1))
+        xtp = ctx.enter_context(tc.psum_pool(name="xtp", bufs=2))
+        o0pp = ctx.enter_context(tc.psum_pool(name="o0pp", bufs=2))
+        ctx.enter_context(tc.manual_schedule())
+
+        z_sb = [[raw.tile([P, 2, CH], F32, name="z%d%d" % (c, a)) for a in range(2)] for c in range(NCH)]
+        g_sb = [raw.tile([P, PACK, CH], BF16, name="g%d" % c) for c in range(NCH)]
+        h_sb = [raw.tile([P, PACK, CH], BF16, name="h%d" % c) for c in range(NCH)]
+        w_sb = raw.tile([P, PACK, CH], BF16, name="w")
+
+        def load_zg(c):
+            nc.sync.dma_start(out=g_sb[c][:], in_=g_v[:, c, :, :])
+            for a in range(2):
+                nc.sync.dma_start(out=z_sb[c][a][:], in_=z_v[:, c, 2 * a : 2 * a + 2, :])
+
+        nc.sync.dma_start(out=h_sb[0][:], in_=h_v[:, 0, :, :])
+        nc.sync.dma_start(out=w_sb[:], in_=w_v)
+        for c in range(NCH):
+            load_zg(c)
+            if c + 1 < NCH:
+                nc.sync.dma_start(out=h_sb[c + 1][:], in_=h_v[:, c + 1, :, :])
+
+        ident = keep.tile([P, P], F32, name="ident")
+        make_identity(nc, ident[:])
+
+        d_sb = [keep.tile([P, PACK, CH], BF16, name="d%d" % c) for c in range(NCH)]
+        ha = [keep.tile([P, CH, PACK], BF16, name="ha%d" % c, align_bytes=64) for c in range(NCH)]
+        wa = keep.tile([P, CH, PACK], BF16, name="wa", align_bytes=64)
+        c_a = [keep.tile([P, CH], U32, name="ca%d" % c, align_bytes=64) for c in range(NCH)]
+        s_a = [keep.tile([P, CH], U8, name="sa%d" % c, align_bytes=64) for c in range(NCH)]
+        c_h = [keep.tile([P, CH], U32, name="ch%d" % c, align_bytes=64) for c in range(NCH)]
+        s_h = [keep.tile([P, CH], U8, name="sh%d" % c, align_bytes=64) for c in range(NCH)]
+        c_w = keep.tile([P, CH], U32, name="cw", align_bytes=64)
+        s_w = keep.tile([P, CH], U8, name="sw", align_bytes=64)
+        c_b = [[keep.tile([P, 2 * P], U32, name="cb%d%d" % (c, a), align_bytes=64) for a in range(2)] for c in range(NCH)]
+        s_b = [[keep.tile([P, 2 * P], U8, name="sb%d%d" % (c, a), align_bytes=64) for a in range(2)] for c in range(NCH)]
+        o0s = [[keep.tile([P, 2, CH], F32, name="o0s%d%d" % (c, a)) for a in range(2)] for c in range(NCH)]
+        o1s = [keep.tile([P, CH], F32, name="o1s%d" % t) for t in range(PACK)]
+        acc = [accp.tile([P, CH], F32, name="acc%d" % t) for t in range(PACK)]
+        xts = {}
+        bts = {}
+        das = {}
+
+        def mask(c, a):
+            nc.vector.scalar_tensor_tensor(
+                out=d_sb[c][:, 2 * a : 2 * a + 2, :],
+                in0=z_sb[c][a][:],
+                scalar=0.0,
+                in1=g_sb[c][:, 2 * a : 2 * a + 2, :],
+                op0=ALU.is_gt,
+                op1=ALU.mult,
+            )
+
+        def turn(c, a):
+            xt = xtp.tile([P, 2, 2, P], F32, name="xt")
+            xts[(c, a)] = xt
+            words = d_sb[c][:].bitcast(F32)
+            for jj in range(2):
+                for u in range(2):
+                    nc.tensor.transpose(xt[:, jj, u, :], words[:, 2 * a + jj, u : CH // 2 : 2], ident[:])
+
+        def turned_out(c, a):
+            bt = rot.tile([P, 2, P, PACK], BF16, name="bt", align_bytes=64, bufs=3)
+            bts[(c, a)] = bt
+            nc.scalar.copy(out=bt[:].bitcast(F32), in_=xts[(c, a)][:].rearrange("p a u r -> p a r u"))
+
+        def quant_b(c, a):
+            nc.vector.quantize_mx(
+                out=c_b[c][a][:].bitcast(E5),
+                scales=s_b[c][a][:],
+                in_=bts[(c, a)][:].rearrange("p a r t -> p (a r t)"),
+            )
+
+        def weave_h(c, half):
+            cols = slice(half * HALF, (half + 1) * HALF)
+            nc.scalar.copy(out=ha[c][:, cols, :], in_=h_sb[c][:, :, cols].rearrange("p j w -> p w j"))
+
+        def quant_h(c):
+            nc.vector.quantize_mx(
+                out=c_h[c][:].bitcast(E4), scales=s_h[c][:], in_=ha[c][:].rearrange("p w j -> p (w j)")
+            )
+
+        def weave_d(c):
+            da = rot.tile([P, CH, PACK], BF16, name="da", align_bytes=64)
+            das[c] = da
+            nc.vector.tensor_copy(out=da[:], in_=d_sb[c][:].rearrange("p j w -> p w j"))
+
+        def quant_a(c):
+            nc.vector.quantize_mx(
+                out=c_a[c][:].bitcast(E5), scales=s_a[c][:], in_=das[c][:].rearrange("p w j -> p (w j)")
+            )
+
+        pss = {}
+
+        def grad_h(c, a):
+            for jj in range(2):
+                ps = o0pp.tile([P, CH], F32, name="ps")
+                pss[(c, a, jj)] = ps
+                cols = slice(jj * P, (jj + 1) * P)
+                nc.tensor.matmul_mx(
+                    out=ps[:],
+                    lhsT=c_b[c][a][:, cols].bitcast(E5),
+                    lhsT_scale=s_b[c][a][:, cols],
+                    rhs=c_w[:].bitcast(E4),
+                    rhs_scale=s_w[:],
+                    start=True,
+                    stop=True,
+                )
+
+        def grad_h_out(c, a):
+            for jj in range(2):
+                nc.scalar.copy(out=o0s[c][a][:, jj, :], in_=pss[(c, a, jj)][:])
+            nc.sync.dma_start(out=o0_v[:, c, 2 * a : 2 * a + 2, :], in_=o0s[c][a][:])
+
+        def grad_w(c, t):
+            cols = slice(t * P, (t + 1) * P)
+            nc.tensor.matmul_mx(
+                out=acc[t][:],
+                lhsT=c_a[c][:, cols].bitcast(E5),
+                lhsT_scale=s_a[c][:, cols],
+                rhs=c_h[c][:].bitcast(E4),
+                rhs_scale=s_h[c][:],
+                start=(c == 0),
+                stop=(c == NCH - 1),
+            )
+
+        weave_h(0, 0)
+        weave_h(0, 1)
+        nc.vector.tensor_copy(out=wa[:], in_=w_sb[:].rearrange("p j w -> p w j"))
+        nc.vector.quantize_mx(out=c_w[:].bitcast(E4), scales=s_w[:], in_=wa[:].rearrange("p w j -> p (w j)"))
+        NH = 2 * NCH
+        for k in range(NH + 1):
+            c, a = divmod(k, 2)
+            if k < NH:
+                mask(c, a)
+                turn(c, a)
+            if a == 1 and 1 <= c < NCH:
+                grad_w(c - 1, 2)
+                grad_w(c - 1, 3)
+            if k < NH:
+                turned_out(c, a)
+            if 1 <= k <= NH:
+                quant_b((k - 1) // 2, (k - 1) % 2)
+                grad_h((k - 1) // 2, (k - 1) % 2)
+            if a == 0 and c >= 1:
+                quant_h(c - 1)
+            if a == 1 and c < NCH:
+                weave_d(c)
+            if 1 <= k <= NH:
+                grad_h_out((k - 1) // 2, (k - 1) % 2)
+            if c + 1 < NCH:
+                weave_h(c + 1, a)
+            if a == 0 and c >= 1:
+                quant_a(c - 1)
+                grad_w(c - 1, 0)
+                grad_w(c - 1, 1)
+        grad_w(NCH - 1, 2)
+        grad_w(NCH - 1, 3)
+        for t in range(PACK):
+            if t % 2 == 0:
+                nc.vector.tensor_copy(out=o1s[t][:], in_=acc[t][:])
+            else:
+                nc.scalar.copy(out=o1s[t][:], in_=acc[t][:])
+            nc.sync.dma_start(out=o1_v[:, t, :], in_=o1s[t][:])

@@ -111,7 +111,10 @@ def tile_gcnstacking_pb_v_kernel(tc, A, msg, h, Ws, b, z, grad_out, out_0, out_1
 
         def weave_h(c, half):
             cols = slice(half * HALF, (half + 1) * HALF)
-            nc.scalar.copy(out=ha[c][:, cols, :], in_=h_sb[c][:, :, cols].rearrange("p j w -> p w j"))
+            nc.scalar.copy(
+                out=ha[c][:, cols, :].rearrange("p (v i) j -> p v j i", i=PACK),
+                in_=h_sb[c][:, :, cols].rearrange("p j (v i) -> p v j i", i=PACK),
+            )
 
         def quant_h(c):
             nc.vector.quantize_mx(
@@ -121,7 +124,10 @@ def tile_gcnstacking_pb_v_kernel(tc, A, msg, h, Ws, b, z, grad_out, out_0, out_1
         def weave_d(c):
             da = rot.tile([P, CH, PACK], BF16, name="da", align_bytes=64)
             das[c] = da
-            nc.vector.tensor_copy(out=da[:], in_=d_sb[c][:].rearrange("p j w -> p w j"))
+            nc.vector.tensor_copy(
+                out=da[:].rearrange("p (v i) j -> p v j i", i=PACK),
+                in_=d_sb[c][:].rearrange("p j (v i) -> p v j i", i=PACK),
+            )
 
         def quant_a(c):
             nc.vector.quantize_mx(
@@ -148,7 +154,10 @@ def tile_gcnstacking_pb_v_kernel(tc, A, msg, h, Ws, b, z, grad_out, out_0, out_1
         def grad_h_out(c, a):
             for jj in range(2):
                 nc.scalar.copy(out=o0s[c][a][:, jj, :], in_=pss[(c, a, jj)][:])
-            nc.sync.dma_start(out=o0_v[:, c, 2 * a : 2 * a + 2, :], in_=o0s[c][a][:])
+                if c == NCH - 1:
+                    nc.sync.dma_start(out=o0_v[:, c, 2 * a + jj, :], in_=o0s[c][a][:, jj, :])
+            if c < NCH - 1:
+                nc.sync.dma_start(out=o0_v[:, c, 2 * a : 2 * a + 2, :], in_=o0s[c][a][:])
 
         def grad_w(c, t):
             cols = slice(t * P, (t + 1) * P)
@@ -164,7 +173,10 @@ def tile_gcnstacking_pb_v_kernel(tc, A, msg, h, Ws, b, z, grad_out, out_0, out_1
 
         weave_h(0, 0)
         weave_h(0, 1)
-        nc.vector.tensor_copy(out=wa[:], in_=w_sb[:].rearrange("p j w -> p w j"))
+        nc.vector.tensor_copy(
+            out=wa[:].rearrange("p (v i) j -> p v j i", i=PACK),
+            in_=w_sb[:].rearrange("p j (v i) -> p v j i", i=PACK),
+        )
         nc.vector.quantize_mx(out=c_w[:].bitcast(E4), scales=s_w[:], in_=wa[:].rearrange("p w j -> p (w j)"))
         NH = 2 * NCH
         for k in range(NH + 1):

@@ -129,10 +129,16 @@ def tile_gcnstacking_pb_v_kernel(tc, A, msg, h, Ws, b, z, grad_out, out_0, out_1
                 in_=d_sb[c][:].rearrange("p j (v i) -> p v j i", i=PACK),
             )
 
-        def quant_a(c):
+        def quant_a(c, half):
+            cols = slice(half * HALF, (half + 1) * HALF)
             nc.vector.quantize_mx(
-                out=c_a[c][:].bitcast(E5), scales=s_a[c][:], in_=das[c][:].rearrange("p w j -> p (w j)")
+                out=c_a[c][:, cols].bitcast(E5),
+                scales=s_a[c][:, cols],
+                in_=das[c][:, cols, :].rearrange("p w j -> p (w j)"),
             )
+
+        def warm(src, t):
+            nc.tensor.matmul(out=acc[t][:], lhsT=src[:, 0, 0:P], rhs=src[:, 0, :], start=True, stop=True)
 
         pss = {}
 
@@ -171,6 +177,9 @@ def tile_gcnstacking_pb_v_kernel(tc, A, msg, h, Ws, b, z, grad_out, out_0, out_1
                 stop=(c == NCH - 1),
             )
 
+        for src in (h_sb[0], w_sb, g_sb[0]):
+            for t in range(3):
+                warm(src, t)
         weave_h(0, 0)
         weave_h(0, 1)
         nc.vector.tensor_copy(
@@ -184,26 +193,27 @@ def tile_gcnstacking_pb_v_kernel(tc, A, msg, h, Ws, b, z, grad_out, out_0, out_1
             if k < NH:
                 mask(c, a)
                 turn(c, a)
-            if a == 1 and 1 <= c < NCH:
-                grad_w(c - 1, 2)
-                grad_w(c - 1, 3)
+            if k == 0:
+                warm(d_sb[0], 0)
+                warm(d_sb[0], 1)
             if k < NH:
                 turned_out(c, a)
-            if 1 <= k <= NH:
+            if k >= 1:
                 quant_b((k - 1) // 2, (k - 1) % 2)
                 grad_h((k - 1) // 2, (k - 1) % 2)
             if a == 0 and c >= 1:
                 quant_h(c - 1)
-            if a == 1 and c < NCH:
+            if a == 1:
                 weave_d(c)
-            if 1 <= k <= NH:
+            if k >= 1:
                 grad_h_out((k - 1) // 2, (k - 1) % 2)
             if c + 1 < NCH:
                 weave_h(c + 1, a)
-            if a == 0 and c >= 1:
-                quant_a(c - 1)
-                grad_w(c - 1, 0)
-                grad_w(c - 1, 1)
+            if c >= 1:
+                quant_a(c - 1, a)
+                grad_w(c - 1, 2 * a)
+                grad_w(c - 1, 2 * a + 1)
+        quant_a(NCH - 1, 1)
         grad_w(NCH - 1, 2)
         grad_w(NCH - 1, 3)
         for t in range(PACK):

@@ -177,8 +177,8 @@ def tile_gcnstacking_pb_v_kernel(tc, A, msg, h, Ws, b, z, grad_out, out_0, out_1
                 stop=(c == NCH - 1),
             )
 
-        for src in (h_sb[0], w_sb, g_sb[0]):
-            for t in range(3):
+        for src, times in ((h_sb[0], 3), (w_sb, 2), (g_sb[0], 2)):
+            for t in range(times):
                 warm(src, t)
         weave_h(0, 0)
         weave_h(0, 1)
@@ -205,6 +205,15 @@ def tile_gcnstacking_pb_v_kernel(tc, A, msg, h, Ws, b, z, grad_out, out_0, out_1
                 quant_h(c - 1)
             if a == 1:
                 weave_d(c)
+            if k == 1:
+                for t in range(3):
+                    nc.tensor.matmul(
+                        out=acc[t][:],
+                        lhsT=das[0][:, 0 : P // PACK, :].rearrange("p w j -> p (w j)"),
+                        rhs=das[0][:, 0:P, :].rearrange("p w j -> p (w j)"),
+                        start=True,
+                        stop=True,
+                    )
             if k >= 1:
                 grad_h_out((k - 1) // 2, (k - 1) % 2)
             if c + 1 < NCH:

@@ -137,8 +137,6 @@ def tile_gcnstacking_pb_v_kernel(tc, A, msg, h, Ws, b, z, grad_out, out_0, out_1
                 in_=das[c][:, cols, :].rearrange("p w j -> p (w j)"),
             )
 
-        def warm(src, t):
-            nc.tensor.matmul(out=acc[t][:], lhsT=src[:, 0, 0:P], rhs=src[:, 0, :], start=True, stop=True)
 
         pss = {}
 
@@ -177,9 +175,6 @@ def tile_gcnstacking_pb_v_kernel(tc, A, msg, h, Ws, b, z, grad_out, out_0, out_1
                 stop=(c == NCH - 1),
             )
 
-        for src, times in ((h_sb[0], 3), (w_sb, 2), (g_sb[0], 2)):
-            for t in range(times):
-                warm(src, t)
         weave_h(0, 0)
         weave_h(0, 1)
         nc.vector.tensor_copy(
@@ -193,9 +188,6 @@ def tile_gcnstacking_pb_v_kernel(tc, A, msg, h, Ws, b, z, grad_out, out_0, out_1
             if k < NH:
                 mask(c, a)
                 turn(c, a)
-            if k == 0:
-                warm(d_sb[0], 0)
-                warm(d_sb[0], 1)
             if k < NH:
                 turned_out(c, a)
             if k >= 1:
@@ -205,15 +197,6 @@ def tile_gcnstacking_pb_v_kernel(tc, A, msg, h, Ws, b, z, grad_out, out_0, out_1
                 quant_h(c - 1)
             if a == 1:
                 weave_d(c)
-            if k == 1:
-                for t in range(3):
-                    nc.tensor.matmul(
-                        out=acc[t][:],
-                        lhsT=das[0][:, 0 : P // PACK, :].rearrange("p w j -> p (w j)"),
-                        rhs=das[0][:, 0:P, :].rearrange("p w j -> p (w j)"),
-                        start=True,
-                        stop=True,
-                    )
             if k >= 1:
                 grad_h_out((k - 1) // 2, (k - 1) % 2)
             if c + 1 < NCH:

from contextlib import ExitStack

import concourse.mybir as mybir
from concourse.masks import make_identity

NODES = 2048
CH = 512
FLOPS = 2 * 2 * NODES * CH * CH
BYTES = NODES * CH * (2 + 4 + 2) + CH * CH * 2 + NODES * CH * 4 + CH * CH * 4

F32 = mybir.dt.float32
BF16 = mybir.dt.bfloat16
U32 = mybir.dt.uint32
U8 = mybir.dt.uint8
E4 = mybir.dt.float8_e4m3fn_x4
E5 = mybir.dt.float8_e5m2_x4
ALU = mybir.AluOpType

P = 128
PACK = 4
PASS = P * PACK
NCH = NODES // PASS
HALF = CH // 2


def tile_gcnstacking_pb_v_kernel(tc, A, msg, h, Ws, b, z, grad_out, out_0, out_1):
    nc = tc.nc
    z_v = z.flatten_outer_dims().rearrange("(c p j) w -> p c j w", p=P, j=PACK)
    g_v = grad_out.flatten_outer_dims().rearrange("(c p j) w -> p c j w", p=P, j=PACK)
    h_v = h.flatten_outer_dims().rearrange("(c p j) w -> p c j w", p=P, j=PACK)
    o0_v = out_0.flatten_outer_dims().rearrange("(c p j) w -> p c j w", p=P, j=PACK)
    w_v = Ws.rearrange("(p j) i -> p j i", j=PACK)
    o1_v = out_1.rearrange("(t m) i -> m t i", m=P)

    with ExitStack() as ctx:
        raw = ctx.enter_context(tc.tile_pool(name="raw", bufs=1))
        keep = ctx.enter_context(tc.tile_pool(name="keep", bufs=1))
        rot = ctx.enter_context(tc.tile_pool(name="rot", bufs=2))
        accp = ctx.enter_context(tc.psum_pool(name="accp", bufs=1))
        xtp = ctx.enter_context(tc.psum_pool(name="xtp", bufs=2))
        o0pp = ctx.enter_context(tc.psum_pool(name="o0pp", bufs=2))
        ctx.enter_context(tc.manual_schedule())

        z_sb = [[raw.tile([P, 2, CH], F32, name="z%d%d" % (c, a)) for a in range(2)] for c in range(NCH)]
        g_sb = [raw.tile([P, PACK, CH], BF16, name="g%d" % c) for c in range(NCH)]
        h_sb = [raw.tile([P, PACK, CH], BF16, name="h%d" % c) for c in range(NCH)]
        w_sb = raw.tile([P, PACK, CH], BF16, name="w")

        def load_zg(c):
            nc.sync.dma_start(out=g_sb[c][:], in_=g_v[:, c, :, :])
            for a in range(2):
                nc.sync.dma_start(out=z_sb[c][a][:], in_=z_v[:, c, 2 * a : 2 * a + 2, :])

        nc.sync.dma_start(out=h_sb[0][:], in_=h_v[:, 0, :, :])
        nc.sync.dma_start(out=w_sb[:], in_=w_v)
        for c in range(NCH):
            load_zg(c)
            if c + 1 < NCH:
                nc.sync.dma_start(out=h_sb[c + 1][:], in_=h_v[:, c + 1, :, :])

        ident = keep.tile([P, P], F32, name="ident")
        make_identity(nc, ident[:])

        d_sb = [keep.tile([P, PACK, CH], BF16, name="d%d" % c) for c in range(NCH)]
        ha = [keep.tile([P, CH, PACK], BF16, name="ha%d" % c, align_bytes=64) for c in range(NCH)]
        wa = keep.tile([P, CH, PACK], BF16, name="wa", align_bytes=64)
        c_a = [keep.tile([P, CH], U32, name="ca%d" % c, align_bytes=64) for c in range(NCH)]
        s_a = [keep.tile([P, CH], U8, name="sa%d" % c, align_bytes=64) for c in range(NCH)]
        c_h = [keep.tile([P, CH], U32, name="ch%d" % c, align_bytes=64) for c in range(NCH)]
        s_h = [keep.tile([P, CH], U8, name="sh%d" % c, align_bytes=64) for c in range(NCH)]
        c_w = keep.tile([P, CH], U32, name="cw", align_bytes=64)
        s_w = keep.tile([P, CH], U8, name="sw", align_bytes=64)
        c_b = [[keep.tile([P, 2 * P], U32, name="cb%d%d" % (c, a), align_bytes=64) for a in range(2)] for c in range(NCH)]
        s_b = [[keep.tile([P, 2 * P], U8, name="sb%d%d" % (c, a), align_bytes=64) for a in range(2)] for c in range(NCH)]
        o0s = [[keep.tile([P, 2, CH], F32, name="o0s%d%d" % (c, a)) for a in range(2)] for c in range(NCH)]
        o1s = [keep.tile([P, CH], F32, name="o1s%d" % t) for t in range(PACK)]
        acc = [accp.tile([P, CH], F32, name="acc%d" % t) for t in range(PACK)]
        xts = {}
        bts = {}
        das = {}

        def mask(c, a):
            nc.vector.scalar_tensor_tensor(
                out=d_sb[c][:, 2 * a : 2 * a + 2, :],
                in0=z_sb[c][a][:],
                scalar=0.0,
                in1=g_sb[c][:, 2 * a : 2 * a + 2, :],
                op0=ALU.is_gt,
                op1=ALU.mult,
            )

        def turn(c, a):
            xt = xtp.tile([P, 2, 2, P], F32, name="xt")
            xts[(c, a)] = xt
            words = d_sb[c][:].bitcast(F32)
            for jj in range(2):
                for u in range(2):
                    nc.tensor.transpose(xt[:, jj, u, :], words[:, 2 * a + jj, u : CH // 2 : 2], ident[:])

        def turned_out(c, a):
            bt = rot.tile([P, 2, P, PACK], BF16, name="bt", align_bytes=64, bufs=3)
            bts[(c, a)] = bt
            nc.scalar.copy(out=bt[:].bitcast(F32), in_=xts[(c, a)][:].rearrange("p a u r -> p a r u"))

        def quant_b(c, a):
            nc.vector.quantize_mx(
                out=c_b[c][a][:].bitcast(E5),
                scales=s_b[c][a][:],
                in_=bts[(c, a)][:].rearrange("p a r t -> p (a r t)"),
            )

        def weave_h(c, half):
            cols = slice(half * HALF, (half + 1) * HALF)
            nc.scalar.copy(
                out=ha[c][:, cols, :].rearrange("p (v i) j -> p v j i", i=PACK),
                in_=h_sb[c][:, :, cols].rearrange("p j (v i) -> p v j i", i=PACK),
            )

        def quant_h(c):
            nc.vector.quantize_mx(
                out=c_h[c][:].bitcast(E4), scales=s_h[c][:], in_=ha[c][:].rearrange("p w j -> p (w j)")
            )

        def weave_d(c):
            da = rot.tile([P, CH, PACK], BF16, name="da", align_bytes=64)
            das[c] = da
            nc.vector.tensor_copy(
                out=da[:].rearrange("p (v i) j -> p v j i", i=PACK),
                in_=d_sb[c][:].rearrange("p j (v i) -> p v j i", i=PACK),
            )

        def quant_a(c, half):
            cols = slice(half * HALF, (half + 1) * HALF)
            nc.vector.quantize_mx(
                out=c_a[c][:, cols].bitcast(E5),
                scales=s_a[c][:, cols],
                in_=das[c][:, cols, :].rearrange("p w j -> p (w j)"),
            )


        pss = {}

        def grad_h(c, a):
            for jj in range(2):
                ps = o0pp.tile([P, CH], F32, name="ps")
                pss[(c, a, jj)] = ps
                cols = slice(jj * P, (jj + 1) * P)
                nc.tensor.matmul_mx(
                    out=ps[:],
                    lhsT=c_b[c][a][:, cols].bitcast(E5),
                    lhsT_scale=s_b[c][a][:, cols],
                    rhs=c_w[:].bitcast(E4),
                    rhs_scale=s_w[:],
                    start=True,
                    stop=True,
                )

        def grad_h_out(c, a):
            for jj in range(2):
                nc.scalar.copy(out=o0s[c][a][:, jj, :], in_=pss[(c, a, jj)][:])
                if c == NCH - 1:
                    nc.sync.dma_start(out=o0_v[:, c, 2 * a + jj, :], in_=o0s[c][a][:, jj, :])
            if c < NCH - 1:
                nc.sync.dma_start(out=o0_v[:, c, 2 * a : 2 * a + 2, :], in_=o0s[c][a][:])

        def grad_w(c, t):
            cols = slice(t * P, (t + 1) * P)
            nc.tensor.matmul_mx(
                out=acc[t][:],
                lhsT=c_a[c][:, cols].bitcast(E5),
                lhsT_scale=s_a[c][:, cols],
                rhs=c_h[c][:].bitcast(E4),
                rhs_scale=s_h[c][:],
                start=(c == 0),
                stop=(c == NCH - 1),
            )

        weave_h(0, 0)
        weave_h(0, 1)
        nc.vector.tensor_copy(
            out=wa[:].rearrange("p (v i) j -> p v j i", i=PACK),
            in_=w_sb[:].rearrange("p j (v i) -> p v j i", i=PACK),
        )
        nc.vector.quantize_mx(out=c_w[:].bitcast(E4), scales=s_w[:], in_=wa[:].rearrange("p w j -> p (w j)"))
        NH = 2 * NCH
        for k in range(NH + 1):
            c, a = divmod(k, 2)
            if k < NH:
                mask(c, a)
                turn(c, a)
            if k < NH:
                turned_out(c, a)
            if k >= 1:
                quant_b((k - 1) // 2, (k - 1) % 2)
                grad_h((k - 1) // 2, (k - 1) % 2)
            if a == 0 and c >= 1:
                quant_h(c - 1)
            if a == 1:
                weave_d(c)
            if k >= 1:
                grad_h_out((k - 1) // 2, (k - 1) % 2)
            if c + 1 < NCH:
                weave_h(c + 1, a)
            if c >= 1:
                quant_a(c - 1, a)
                grad_w(c - 1, 2 * a)
                grad_w(c - 1, 2 * a + 1)
        quant_a(NCH - 1, 1)
        grad_w(NCH - 1, 2)
        grad_w(NCH - 1, 3)
        for t in range(PACK):
            if t % 2 == 0:
                nc.vector.tensor_copy(out=o1s[t][:], in_=acc[t][:])
            else:
                nc.scalar.copy(out=o1s[t][:], in_=acc[t][:])
            nc.sync.dma_start(out=o1_v[:, t, :], in_=o1s[t][:])
